import numpy as np
import ml_dtypes


def mxq(x, axis, fmt="e4m3"):
    dtype, down = {"e4m3": (ml_dtypes.float8_e4m3fn, 7), "e5m2": (ml_dtypes.float8_e5m2, 14)}[fmt]
    v = np.moveaxis(np.asarray(x, np.float32).astype(ml_dtypes.bfloat16).astype(np.float64), axis, -1)
    blocks = v.reshape(v.shape[:-1] + (-1, 32))
    amax = np.abs(blocks).max(-1, keepdims=True)
    byte = np.maximum(np.where(amax > 0, np.frexp(amax)[1] - 1 + 127, 0) - down, 1)
    scale = np.exp2(byte - 127.0)
    codes = (blocks / scale).astype(np.float32).astype(dtype).astype(np.float64)
    return np.moveaxis((codes * scale).reshape(v.shape), -1, axis)


WIDE = False


def mx_kscale(k):
    if not WIDE:
        return np.ones(k)
    levels = np.array([10, -10, 5, -5, 0])
    a = np.random.permutation(np.resize(levels, k // 512 * 4)).reshape(k // 512, 4)
    idx = np.arange(k)
    return np.exp2(a[idx // 512, idx % 128 // 32])


BF16 = ml_dtypes.bfloat16


def bf(x):
    return np.asarray(x, np.float32).astype(BF16)


def f64(x):
    return np.asarray(x).astype(np.float64)


E2M1 = np.array([0.0, 0.5, 1.0, 1.5, 2.0, 3.0, 4.0, 6.0, -0.0, -0.5, -1.0, -1.5, -2.0, -3.0, -4.0, -6.0])


def pack_weight(w, fmt):
    k, n = w.shape
    w = f64(bf(w)).reshape(k // 32, 32, n)
    amax = np.abs(w).max(1)
    if fmt == "e4m3":
        byte = np.frexp(amax)[1] - 1 + 127 - 7
    else:
        mant, ex = np.frexp(amax / 6.0)
        byte = np.where(mant > 0.5, ex, ex - 1) + 127
    byte = np.clip(np.where(amax > 0, byte, 1), 1, 254)
    scaled = (w * np.exp2(127.0 - byte)[:, None, :]).reshape(k, n).astype(np.float32)
    by_word = np.ascontiguousarray(scaled.reshape(k // 512, 128, 4, n).transpose(0, 1, 3, 2))
    if fmt == "e4m3":
        words = by_word.astype(ml_dtypes.float8_e4m3fn).view(np.uint8)
    else:
        c = by_word.astype(ml_dtypes.float4_e2m1fn).view(np.uint8) & 0xF
        words = c[..., 0::2] | (c[..., 1::2] << 4)
    return np.ascontiguousarray(words), np.ascontiguousarray(byte.astype(np.uint8).reshape(k // 512, 16, n))


def unpack_weight(words, scales, fmt):
    g, p, n, _ = words.shape
    if fmt == "e4m3":
        vals = np.ascontiguousarray(words).view(ml_dtypes.float8_e4m3fn).astype(np.float64)
    else:
        nib = np.empty((g, p, n, 4), np.uint8)
        nib[..., 0::2] = words & 0xF
        nib[..., 1::2] = words >> 4
        vals = E2M1[nib]
    vals = vals * np.repeat(np.exp2(scales.astype(np.float64) - 127.0), 8, axis=1)[..., None]
    return vals.transpose(0, 1, 3, 2).reshape(g * 512, n)


B, T, D, S, R = 2, 512, 2048, 8, 64
EPS = float(np.finfo(np.float32).eps)


def silu(v):
    return v / (1.0 + np.exp(-v))


def sigmoid(v):
    return 1.0 / (1.0 + np.exp(-v))


def setup_inputs():
    g = 0.5 + 1.5 * np.random.random((B, T, 1))
    g[:, ::4] *= 2.0 ** -12
    s = mx_kscale(D)
    c = 2.0 ** np.round(np.log2(np.sqrt(np.mean(s * s))))
    h = bf(np.random.standard_normal((B, T, D)) * g * s / c)
    w_down = np.random.standard_normal((S, R, D)) * 1.5 / np.sqrt(D) * c / s
    cat = np.ascontiguousarray(w_down.swapaxes(1, 2)).reshape(-1, R)
    words, scales = pack_weight(cat, "e4m3")
    return {"h": h,
            "w_down_words": words,
            "w_down_scales": scales,
            "w_up": bf(np.random.standard_normal((S, D, R)) * S / np.sqrt(S * R)),
            "gate_bias": bf(0.8 + 0.1 * np.random.standard_normal(1))}


def reference(h, w_down_words, w_down_scales, w_up, gate_bias):
    h64 = f64(h)
    rms = np.sqrt(np.mean(h64 * h64, axis=-1, keepdims=True) + EPS)
    h_norm = h64 / rms
    a = mxq(h_norm, 2, "e4m3") @ unpack_weight(w_down_words, w_down_scales, "e4m3").reshape(S, D, R).transpose(1, 0, 2).reshape(D, S * R)
    view = silu(a)
    upd = mxq(view, 2, "e4m3") @ mxq(f64(w_up).transpose(0, 2, 1).reshape(S * R, D), 0, "e4m3")
    mean_update = upd / S
    gate = sigmoid(f64(gate_bias))
    return h64 + gate * mean_update

@@ -1,0 +1,212 @@
+from contextlib import ExitStack
+
+import concourse.mybir as mybir
+from concourse.masks import make_identity
+
+BF16 = mybir.dt.bfloat16
+F32 = mybir.dt.float32
+I32 = mybir.dt.int32
+U32 = mybir.dt.uint32
+U8 = mybir.dt.uint8
+FP8X4 = mybir.dt.float8_e4m3fn_x4
+ACT = mybir.ActivationFunctionType
+ALU = mybir.AluOpType
+
+P = 128
+PACK = 4
+K_PASS = P * PACK
+TOKENS = 1024
+D_MODEL = 2048
+SPOKES = 8
+RANK = 64
+PAIRS = SPOKES * RANK
+TOKEN_TILES = TOKENS // P
+DOWN_PASSES = D_MODEL // K_PASS
+PAIR_TILES = PAIRS // P
+D_CHUNK = 512
+D_CHUNKS = D_MODEL // D_CHUNK
+ROWS_PER_PARTITION = D_MODEL // P
+EPS = 2.0 ** -23
+BACK_LAG = 3
+W_UP_ROUND = 2
+
+FLOPS = 2 * TOKENS * D_MODEL * PAIRS * 2
+
+
+def tile_spokelayer_e_kernel(tc, h, w_down_words, w_down_scales, w_up, gate_bias, out):
+    nc = tc.nc
+    h_rows = h.flatten_outer_dims()
+    out_rows = out.flatten_outer_dims()
+
+    with ExitStack() as ctx:
+        keep = ctx.enter_context(tc.tile_pool(name="keep", bufs=1))
+        work = ctx.enter_context(tc.tile_pool(name="work", bufs=2))
+        results = ctx.enter_context(tc.tile_pool(name="results", bufs=3))
+        turned_banks = ctx.enter_context(tc.psum_pool(name="turned_banks", bufs=3))
+        down_banks = ctx.enter_context(tc.psum_pool(name="down_banks", bufs=2))
+        up_banks = ctx.enter_context(tc.psum_pool(name="up_banks", bufs=3))
+
+        ident_f32 = keep.tile([P, P], F32)
+        make_identity(nc, ident_f32[:])
+        ident_bf16 = keep.tile([P, P], BF16)
+        make_identity(nc, ident_bf16[:])
+        minus_half = keep.tile([P, 1], F32)
+        nc.gpsimd.memset(minus_half[:], -0.5)
+
+        h_sb = []
+        for i in range(TOKEN_TILES):
+            h_tile = keep.tile([P, D_MODEL], BF16, name="h%d" % i)
+            h_sb.append(h_tile)
+
+        def load_tokens(i):
+            nc.sync.dma_start(out=h_sb[i][:], in_=h_rows[i * P:(i + 1) * P, :])
+
+        gate_raw = keep.tile([P, 1], BF16)
+        nc.sync.dma_start(out=gate_raw[:], in_=gate_bias.partition_broadcast(P))
+        load_tokens(0)
+        load_tokens(1)
+
+        wu_raw = keep.tile([P, SPOKES, ROWS_PER_PARTITION * RANK], BF16)
+        wu_dram = w_up.rearrange("s (p j) r -> p s (j r)", j=ROWS_PER_PARTITION)
+        for t in range(PAIR_TILES):
+            nc.sync.dma_start(out=wu_raw[:, 2 * t:2 * t + 2, :], in_=wu_dram[:, 2 * t:2 * t + 2, :])
+
+        wd_scales_raw = keep.tile([P, SPOKES * DOWN_PASSES * RANK], U8, align_bytes=64)
+        nc.vector.memset(wd_scales_raw[:].bitcast(I32), 0)
+        for quadrant in range(4):
+            nc.sync.dma_start(
+                out=wd_scales_raw[32 * quadrant:32 * quadrant + 4, :].bitcast(I32).rearrange("r (g w) -> r g w", w=RANK // 4),
+                in_=w_down_scales[:, 4 * quadrant:4 * quadrant + 4, :].bitcast(I32).rearrange("g r w -> r g w"),
+            )
+        wd_codes = keep.tile([P, DOWN_PASSES, PAIRS], U32, align_bytes=64)
+        wd_dram = w_down_words.rearrange("(s c) p n t -> c p s (n t)", c=DOWN_PASSES).bitcast(I32)
+        for c in range(DOWN_PASSES):
+            nc.sync.dma_start(
+                out=wd_codes[:, c, :].bitcast(I32).rearrange("p (s n) -> p s n", n=RANK),
+                in_=wd_dram[c],
+            )
+        for i in range(2, TOKEN_TILES):
+            load_tokens(i)
+
+        gate_tanh = keep.tile([P, 1], F32)
+        nc.scalar.activation(out=gate_tanh[:], in_=gate_raw[:], func=ACT.Tanh, scale=0.5)
+        gate_eighth = keep.tile([P, 1], F32)
+        nc.vector.tensor_scalar(out=gate_eighth[:], in0=gate_tanh[:], scalar1=1.0, scalar2=0.5 / SPOKES,
+                                op0=ALU.add, op1=ALU.mult)
+
+        wd_scales = keep.tile([P, DOWN_PASSES, PAIRS], U8, align_bytes=64)
+        nc.vector.tensor_copy(
+            out=wd_scales[:].rearrange("p c n -> p (c n)").bitcast(I32).rearrange(
+                "p (c s w) -> p c s w", c=DOWN_PASSES, s=SPOKES),
+            in_=wd_scales_raw[:].bitcast(I32).rearrange("p (s c w) -> p c s w", c=DOWN_PASSES, s=SPOKES),
+        )
+
+        wu_sorted = keep.tile([P, PAIR_TILES, ROWS_PER_PARTITION, P], BF16)
+        wu_grouped = keep.tile([P, D_MODEL, PACK], BF16, align_bytes=64)
+        wu_codes = keep.tile([P, D_MODEL], U32, align_bytes=64)
+        wu_scales = keep.tile([P, D_MODEL], U8, align_bytes=64)
+
+        def prepare_w_up():
+            for t in range(PAIR_TILES):
+                nc.vector.tensor_copy(
+                    out=wu_sorted[:, t, :, :].rearrange("p j (x r) -> p j x r", x=2),
+                    in_=wu_raw[:, 2 * t:2 * t + 2, :].rearrange("p x (j r) -> p j x r", r=RANK),
+                )
+            wu_grouped_rows = wu_grouped[:].rearrange("m (p j) t -> m p j t", j=ROWS_PER_PARTITION)
+            for b in range(ROWS_PER_PARTITION // 2):
+                wu_turned = turned_banks.tile([P, 2, PAIR_TILES, P], BF16, tag="turned")
+                for jj in range(2):
+                    for t in range(PAIR_TILES):
+                        nc.tensor.transpose(out=wu_turned[:, jj, t, :], in_=wu_sorted[:, t, 2 * b + jj, :],
+                                            identity=ident_bf16[:])
+                if (b // 2) % 2 == 0:
+                    nc.scalar.copy(out=wu_grouped_rows[:, :, 2 * b:2 * b + 2, :],
+                                   in_=wu_turned[:].rearrange("m j t p -> m p j t"))
+                else:
+                    nc.vector.tensor_copy(out=wu_grouped_rows[:, :, 2 * b:2 * b + 2, :],
+                                          in_=wu_turned[:].rearrange("m j t p -> m p j t"))
+            for half in range(2):
+                cols = slice(half * D_MODEL // 2, (half + 1) * D_MODEL // 2)
+                nc.vector.quantize_mx(
+                    out=wu_codes[:, cols].bitcast(FP8X4),
+                    scales=wu_scales[:, cols],
+                    in_=wu_grouped[:, cols, :].rearrange("m d t -> m (d t)"),
+                )
+
+        h_codes = keep.tile([P, TOKEN_TILES, DOWN_PASSES * P], U32, align_bytes=64)
+        h_scales = keep.tile([P, TOKEN_TILES, DOWN_PASSES * P], U8, align_bytes=64)
+        view_codes = keep.tile([P, TOKEN_TILES, P], U32, align_bytes=64)
+        view_scales = keep.tile([P, TOKEN_TILES, P], U8, align_bytes=64)
+
+        def down_projection(i):
+            squares = work.tile([P, D_MODEL], BF16, tag="squares")
+            sum_sq = keep.tile([P, 1], F32, name="sum_sq%d" % i)
+            nc.scalar.activation(out=squares[:], in_=h_sb[i][:], func=ACT.Square, accum_out=sum_sq[:])
+            mean_sq = keep.tile([P, 1], F32, name="mean_sq%d" % i)
+            nc.gpsimd.tensor_scalar(out=mean_sq[:], in0=sum_sq[:], scalar1=1.0 / D_MODEL, scalar2=EPS,
+                                    op0=ALU.mult, op1=ALU.add)
+            rstd = keep.tile([P, 1], F32, name="rstd%d" % i)
+            nc.gpsimd.tensor_tensor(out=rstd[:], in0=mean_sq[:], in1=minus_half[:], op=ALU.pow)
+
+            h_norm = work.tile([P, D_MODEL], BF16, tag="h_norm")
+            nc.vector.tensor_scalar(out=h_norm[:], in0=h_sb[i][:], scalar1=rstd[:, 0:1], scalar2=None, op0=ALU.mult)
+
+            h_words = h_norm[:].bitcast(F32)
+            h_grouped = work.tile([P, D_MODEL], BF16, tag="h_grouped", align_bytes=64)
+            h_grouped_words = h_grouped[:].bitcast(F32).rearrange("p (g n u) -> p g n u", g=DOWN_PASSES, u=2)
+            for half in range(2):
+                h_turned = turned_banks.tile([P, 2, 2, P], F32, tag="turned")
+                for gg in range(2):
+                    g = 2 * half + gg
+                    for u in range(2):
+                        nc.tensor.transpose(out=h_turned[:, gg, u, :],
+                                            in_=h_words[:, 256 * g + u:256 * (g + 1):2],
+                                            identity=ident_f32[:])
+                nc.scalar.copy(out=h_grouped_words[:, 2 * half:2 * half + 2, :, :],
+                               in_=h_turned[:].rearrange("p g u n -> p g n u"))
+            nc.vector.quantize_mx(out=h_codes[:, i, :].bitcast(FP8X4), scales=h_scales[:, i, :], in_=h_grouped[:])
+
+            down = down_banks.tile([P, PAIR_TILES, P], F32, tag="down")
+            for t in range(PAIR_TILES):
+                for g in range(DOWN_PASSES):
+                    nc.tensor.matmul_mx(
+                        out=down[:, t, :],
+                        lhsT=wd_codes[:, g, t * P:(t + 1) * P].bitcast(FP8X4),
+                        lhsT_scale=wd_scales[:, g, t * P:(t + 1) * P],
+                        rhs=h_codes[:, i, g * P:(g + 1) * P].bitcast(FP8X4),
+                        rhs_scale=h_scales[:, i, g * P:(g + 1) * P],
+                        start=(g == 0),
+                        stop=(g == DOWN_PASSES - 1),
+                    )
+            view = work.tile([P, P, PACK], BF16, tag="view", align_bytes=64)
+            nc.scalar.activation(out=view[:], in_=down[:].rearrange("m t n -> m n t"), func=ACT.Silu)
+            nc.vector.quantize_mx(out=view_codes[:, i, :].bitcast(FP8X4), scales=view_scales[:, i, :],
+                                  in_=view[:].rearrange("m n t -> m (n t)"))
+
+        def up_projection(i):
+            result = results.tile([P, D_MODEL], F32, tag="result")
+            for c in range(D_CHUNKS):
+                cols = slice(c * D_CHUNK, (c + 1) * D_CHUNK)
+                up = up_banks.tile([P, D_CHUNK], F32, tag="up")
+                nc.tensor.matmul_mx(
+                    out=up[:],
+                    lhsT=view_codes[:, i, :].bitcast(FP8X4),
+                    lhsT_scale=view_scales[:, i, :],
+                    rhs=wu_codes[:, cols].bitcast(FP8X4),
+                    rhs_scale=wu_scales[:, cols],
+                    start=True,
+                    stop=True,
+                )
+                nc.vector.scalar_tensor_tensor(out=result[:, cols], in0=up[:], scalar=gate_eighth[:, 0:1],
+                                               in1=h_sb[i][:, cols], op0=ALU.mult, op1=ALU.add)
+                if c % 2 == 1:
+                    done = slice((c - 1) * D_CHUNK, (c + 1) * D_CHUNK)
+                    nc.sync.dma_start(out=out_rows[i * P:(i + 1) * P, done], in_=result[:, done])
+
+        for n in range(TOKEN_TILES + BACK_LAG):
+            if n == W_UP_ROUND:
+                prepare_w_up()
+            if n < TOKEN_TILES:
+                down_projection(n)
+            if n >= BACK_LAG:
+                up_projection(n - BACK_LAG)

@@ -27,8 +27,7 @@ D_CHUNK = 512
 D_CHUNKS = D_MODEL // D_CHUNK
 ROWS_PER_PARTITION = D_MODEL // P
 EPS = 2.0 ** -23
-BACK_LAG = 3
-W_UP_ROUND = 2
+LEAD = 2
 
 FLOPS = 2 * TOKENS * D_MODEL * PAIRS * 2
 
@@ -43,8 +42,9 @@ def tile_spokelayer_e_kernel(tc, h, w_down_words, w_down_scales, w_up, gate_bias
         work = ctx.enter_context(tc.tile_pool(name="work", bufs=2))
         results = ctx.enter_context(tc.tile_pool(name="results", bufs=3))
         turned_banks = ctx.enter_context(tc.psum_pool(name="turned_banks", bufs=3))
-        down_banks = ctx.enter_context(tc.psum_pool(name="down_banks", bufs=2))
-        up_banks = ctx.enter_context(tc.psum_pool(name="up_banks", bufs=3))
+        down_banks = ctx.enter_context(tc.psum_pool(name="down_banks", bufs=1))
+        up_banks = ctx.enter_context(tc.psum_pool(name="up_banks", bufs=D_CHUNKS))
+        ctx.enter_context(tc.manual_schedule())
 
         ident_f32 = keep.tile([P, P], F32)
         make_identity(nc, ident_f32[:])
@@ -63,8 +63,8 @@ def tile_spokelayer_e_kernel(tc, h, w_down_words, w_down_scales, w_up, gate_bias
 
         gate_raw = keep.tile([P, 1], BF16)
         nc.sync.dma_start(out=gate_raw[:], in_=gate_bias.partition_broadcast(P))
-        load_tokens(0)
-        load_tokens(1)
+        for i in range(LEAD):
+            load_tokens(i)
 
         wu_raw = keep.tile([P, SPOKES, ROWS_PER_PARTITION * RANK], BF16)
         wu_dram = w_up.rearrange("s (p j) r -> p s (j r)", j=ROWS_PER_PARTITION)
@@ -85,7 +85,7 @@ def tile_spokelayer_e_kernel(tc, h, w_down_words, w_down_scales, w_up, gate_bias
                 out=wd_codes[:, c, :].bitcast(I32).rearrange("p (s n) -> p s n", n=RANK),
                 in_=wd_dram[c],
             )
-        for i in range(2, TOKEN_TILES):
+        for i in range(LEAD, TOKEN_TILES):
             load_tokens(i)
 
         gate_tanh = keep.tile([P, 1], F32)
@@ -95,23 +95,26 @@ def tile_spokelayer_e_kernel(tc, h, w_down_words, w_down_scales, w_up, gate_bias
                                 op0=ALU.add, op1=ALU.mult)
 
         wd_scales = keep.tile([P, DOWN_PASSES, PAIRS], U8, align_bytes=64)
-        nc.vector.tensor_copy(
-            out=wd_scales[:].rearrange("p c n -> p (c n)").bitcast(I32).rearrange(
-                "p (c s w) -> p c s w", c=DOWN_PASSES, s=SPOKES),
-            in_=wd_scales_raw[:].bitcast(I32).rearrange("p (s c w) -> p c s w", c=DOWN_PASSES, s=SPOKES),
-        )
+
+        def move_w_down_scales():
+            nc.vector.tensor_copy(
+                out=wd_scales[:].rearrange("p c n -> p (c n)").bitcast(I32).rearrange(
+                    "p (c s w) -> p c s w", c=DOWN_PASSES, s=SPOKES),
+                in_=wd_scales_raw[:].bitcast(I32).rearrange("p (s c w) -> p c s w", c=DOWN_PASSES, s=SPOKES),
+            )
 
         wu_sorted = keep.tile([P, PAIR_TILES, ROWS_PER_PARTITION, P], BF16)
         wu_grouped = keep.tile([P, D_MODEL, PACK], BF16, align_bytes=64)
         wu_codes = keep.tile([P, D_MODEL], U32, align_bytes=64)
         wu_scales = keep.tile([P, D_MODEL], U8, align_bytes=64)
 
-        def prepare_w_up():
-            for t in range(PAIR_TILES):
-                nc.vector.tensor_copy(
-                    out=wu_sorted[:, t, :, :].rearrange("p j (x r) -> p j x r", x=2),
-                    in_=wu_raw[:, 2 * t:2 * t + 2, :].rearrange("p x (j r) -> p j x r", r=RANK),
-                )
+        def sort_w_up(t):
+            nc.vector.tensor_copy(
+                out=wu_sorted[:, t, :, :].rearrange("p j (x r) -> p j x r", x=2),
+                in_=wu_raw[:, 2 * t:2 * t + 2, :].rearrange("p x (j r) -> p j x r", r=RANK),
+            )
+
+        def turn_and_group_w_up():
             wu_grouped_rows = wu_grouped[:].rearrange("m (p j) t -> m p j t", j=ROWS_PER_PARTITION)
             for b in range(ROWS_PER_PARTITION // 2):
                 wu_turned = turned_banks.tile([P, 2, PAIR_TILES, P], BF16, tag="turned")
@@ -125,6 +128,8 @@ def tile_spokelayer_e_kernel(tc, h, w_down_words, w_down_scales, w_up, gate_bias
                 else:
                     nc.vector.tensor_copy(out=wu_grouped_rows[:, :, 2 * b:2 * b + 2, :],
                                           in_=wu_turned[:].rearrange("m j t p -> m p j t"))
+
+        def quantise_w_up():
             for half in range(2):
                 cols = slice(half * D_MODEL // 2, (half + 1) * D_MODEL // 2)
                 nc.vector.quantize_mx(
@@ -137,40 +142,57 @@ def tile_spokelayer_e_kernel(tc, h, w_down_words, w_down_scales, w_up, gate_bias
         h_scales = keep.tile([P, TOKEN_TILES, DOWN_PASSES * P], U8, align_bytes=64)
         view_codes = keep.tile([P, TOKEN_TILES, P], U32, align_bytes=64)
         view_scales = keep.tile([P, TOKEN_TILES, P], U8, align_bytes=64)
+        rstd = {}
+        h_norm = {}
+        h_turned = {}
+        h_grouped = {}
+        down = {}
+        view = {}
+        up = {}
 
-        def down_projection(i):
+        def sum_squares(i):
             squares = work.tile([P, D_MODEL], BF16, tag="squares")
             sum_sq = keep.tile([P, 1], F32, name="sum_sq%d" % i)
             nc.scalar.activation(out=squares[:], in_=h_sb[i][:], func=ACT.Square, accum_out=sum_sq[:])
             mean_sq = keep.tile([P, 1], F32, name="mean_sq%d" % i)
             nc.gpsimd.tensor_scalar(out=mean_sq[:], in0=sum_sq[:], scalar1=1.0 / D_MODEL, scalar2=EPS,
                                     op0=ALU.mult, op1=ALU.add)
-            rstd = keep.tile([P, 1], F32, name="rstd%d" % i)
-            nc.gpsimd.tensor_tensor(out=rstd[:], in0=mean_sq[:], in1=minus_half[:], op=ALU.pow)
+            rstd[i] = keep.tile([P, 1], F32, name="rstd%d" % i)
+            nc.gpsimd.tensor_tensor(out=rstd[i][:], in0=mean_sq[:], in1=minus_half[:], op=ALU.pow)
 
-            h_norm = work.tile([P, D_MODEL], BF16, tag="h_norm")
-            nc.vector.tensor_scalar(out=h_norm[:], in0=h_sb[i][:], scalar1=rstd[:, 0:1], scalar2=None, op0=ALU.mult)
+        def normalise(i):
+            h_norm[i] = work.tile([P, D_MODEL], BF16, tag="h_norm", name="h_norm%d" % i)
+            nc.vector.tensor_scalar(out=h_norm[i][:], in0=h_sb[i][:], scalar1=rstd[i][:, 0:1], scalar2=None,
+                                    op0=ALU.mult)
 
-            h_words = h_norm[:].bitcast(F32)
-            h_grouped = work.tile([P, D_MODEL], BF16, tag="h_grouped", align_bytes=64)
-            h_grouped_words = h_grouped[:].bitcast(F32).rearrange("p (g n u) -> p g n u", g=DOWN_PASSES, u=2)
+        def turn(i):
+            h_words = h_norm[i][:].bitcast(F32)
+            h_turned[i] = []
             for half in range(2):
-                h_turned = turned_banks.tile([P, 2, 2, P], F32, tag="turned")
+                bank = turned_banks.tile([P, 2, 2, P], F32, tag="turned", name="h_turned%d_%d" % (i, half))
+                h_turned[i].append(bank)
                 for gg in range(2):
                     g = 2 * half + gg
                     for u in range(2):
-                        nc.tensor.transpose(out=h_turned[:, gg, u, :],
-                                            in_=h_words[:, 256 * g + u:256 * (g + 1):2],
+                        nc.tensor.transpose(out=bank[:, gg, u, :], in_=h_words[:, 256 * g + u:256 * (g + 1):2],
                                             identity=ident_f32[:])
-                nc.scalar.copy(out=h_grouped_words[:, 2 * half:2 * half + 2, :, :],
-                               in_=h_turned[:].rearrange("p g u n -> p g n u"))
-            nc.vector.quantize_mx(out=h_codes[:, i, :].bitcast(FP8X4), scales=h_scales[:, i, :], in_=h_grouped[:])
 
-            down = down_banks.tile([P, PAIR_TILES, P], F32, tag="down")
+        def collect(i):
+            h_grouped[i] = work.tile([P, D_MODEL], BF16, tag="h_grouped", name="h_grouped%d" % i, align_bytes=64)
+            grouped_words = h_grouped[i][:].bitcast(F32).rearrange("p (g n u) -> p g n u", g=DOWN_PASSES, u=2)
+            for half in range(2):
+                nc.scalar.copy(out=grouped_words[:, 2 * half:2 * half + 2, :, :],
+                               in_=h_turned[i][half][:].rearrange("p g u n -> p g n u"))
+
+        def quantise_h(i):
+            nc.vector.quantize_mx(out=h_codes[:, i, :].bitcast(FP8X4), scales=h_scales[:, i, :], in_=h_grouped[i][:])
+
+        def project_down(i):
+            down[i] = down_banks.tile([P, PAIR_TILES, P], F32, tag="down", name="down%d" % i)
             for t in range(PAIR_TILES):
                 for g in range(DOWN_PASSES):
                     nc.tensor.matmul_mx(
-                        out=down[:, t, :],
+                        out=down[i][:, t, :],
                         lhsT=wd_codes[:, g, t * P:(t + 1) * P].bitcast(FP8X4),
                         lhsT_scale=wd_scales[:, g, t * P:(t + 1) * P],
                         rhs=h_codes[:, i, g * P:(g + 1) * P].bitcast(FP8X4),
@@ -178,18 +200,23 @@ def tile_spokelayer_e_kernel(tc, h, w_down_words, w_down_scales, w_up, gate_bias
                         start=(g == 0),
                         stop=(g == DOWN_PASSES - 1),
                     )
-            view = work.tile([P, P, PACK], BF16, tag="view", align_bytes=64)
-            nc.scalar.activation(out=view[:], in_=down[:].rearrange("m t n -> m n t"), func=ACT.Silu)
-            nc.vector.quantize_mx(out=view_codes[:, i, :].bitcast(FP8X4), scales=view_scales[:, i, :],
-                                  in_=view[:].rearrange("m n t -> m (n t)"))
 
-        def up_projection(i):
-            result = results.tile([P, D_MODEL], F32, tag="result")
+        def silu(i):
+            view[i] = work.tile([P, P, PACK], BF16, tag="view", name="view%d" % i, align_bytes=64)
+            nc.scalar.activation(out=view[i][:], in_=down[i][:].rearrange("m t n -> m n t"), func=ACT.Silu)
+
+        def quantise_view(i):
+            nc.vector.quantize_mx(out=view_codes[:, i, :].bitcast(FP8X4), scales=view_scales[:, i, :],
+                                  in_=view[i][:].rearrange("m n t -> m (n t)"))
+
+        def project_up(i):
+            up[i] = []
             for c in range(D_CHUNKS):
                 cols = slice(c * D_CHUNK, (c + 1) * D_CHUNK)
-                up = up_banks.tile([P, D_CHUNK], F32, tag="up")
+                bank = up_banks.tile([P, D_CHUNK], F32, tag="up", name="up%d_%d" % (i, c))
+                up[i].append(bank)
                 nc.tensor.matmul_mx(
-                    out=up[:],
+                    out=bank[:],
                     lhsT=view_codes[:, i, :].bitcast(FP8X4),
                     lhsT_scale=view_scales[:, i, :],
                     rhs=wu_codes[:, cols].bitcast(FP8X4),
@@ -197,16 +224,55 @@ def tile_spokelayer_e_kernel(tc, h, w_down_words, w_down_scales, w_up, gate_bias
                     start=True,
                     stop=True,
                 )
-                nc.vector.scalar_tensor_tensor(out=result[:, cols], in0=up[:], scalar=gate_eighth[:, 0:1],
+
+        def finish(i):
+            result = results.tile([P, D_MODEL], F32, tag="result")
+            for c in range(D_CHUNKS):
+                cols = slice(c * D_CHUNK, (c + 1) * D_CHUNK)
+                nc.vector.scalar_tensor_tensor(out=result[:, cols], in0=up[i][c][:], scalar=gate_eighth[:, 0:1],
                                                in1=h_sb[i][:, cols], op0=ALU.mult, op1=ALU.add)
                 if c % 2 == 1:
                     done = slice((c - 1) * D_CHUNK, (c + 1) * D_CHUNK)
                     nc.sync.dma_start(out=out_rows[i * P:(i + 1) * P, done], in_=result[:, done])
 
-        for n in range(TOKEN_TILES + BACK_LAG):
-            if n == W_UP_ROUND:
-                prepare_w_up()
-            if n < TOKEN_TILES:
-                down_projection(n)
-            if n >= BACK_LAG:
-                up_projection(n - BACK_LAG)
+        for i in range(LEAD):
+            sum_squares(i)
+        for i in range(LEAD):
+            normalise(i)
+            turn(i)
+            sort_w_up(2 * i)
+            sort_w_up(2 * i + 1)
+        move_w_down_scales()
+        for i in range(LEAD):
+            collect(i)
+            quantise_h(i)
+        turn_and_group_w_up()
+        project_down(0)
+        silu(0)
+        project_down(1)
+        sum_squares(2)
+        quantise_w_up()
+        silu(1)
+        quantise_view(0)
+        quantise_view(1)
+        project_up(0)
+        sum_squares(3)
+        normalise(2)
+        turn(2)
+        finish(0)
+        project_up(1)
+
+        for n in range(LEAD, TOKEN_TILES):
+            collect(n)
+            quantise_h(n)
+            project_down(n)
+            if n + 1 < TOKEN_TILES:
+                normalise(n + 1)
+                turn(n + 1)
+            finish(n - 1)
+            if n + 2 < TOKEN_TILES:
+                sum_squares(n + 2)
+            silu(n)
+            quantise_view(n)
+            project_up(n)
+        finish(TOKEN_TILES - 1)

@@ -27,7 +27,7 @@ D_CHUNK = 512
 D_CHUNKS = D_MODEL // D_CHUNK
 ROWS_PER_PARTITION = D_MODEL // P
 EPS = 2.0 ** -23
-LEAD = 2
+AHEAD = 3
 
 FLOPS = 2 * TOKENS * D_MODEL * PAIRS * 2
 
@@ -63,7 +63,7 @@ def tile_spokelayer_e_kernel(tc, h, w_down_words, w_down_scales, w_up, gate_bias
 
         gate_raw = keep.tile([P, 1], BF16)
         nc.sync.dma_start(out=gate_raw[:], in_=gate_bias.partition_broadcast(P))
-        for i in range(LEAD):
+        for i in range(AHEAD):
             load_tokens(i)
 
         wu_raw = keep.tile([P, SPOKES, ROWS_PER_PARTITION * RANK], BF16)
@@ -85,7 +85,7 @@ def tile_spokelayer_e_kernel(tc, h, w_down_words, w_down_scales, w_up, gate_bias
                 out=wd_codes[:, c, :].bitcast(I32).rearrange("p (s n) -> p s n", n=RANK),
                 in_=wd_dram[c],
             )
-        for i in range(LEAD, TOKEN_TILES):
+        for i in range(AHEAD, TOKEN_TILES):
             load_tokens(i)
 
         gate_tanh = keep.tile([P, 1], F32)
@@ -114,9 +114,9 @@ def tile_spokelayer_e_kernel(tc, h, w_down_words, w_down_scales, w_up, gate_bias
                 in_=wu_raw[:, 2 * t:2 * t + 2, :].rearrange("p x (j r) -> p j x r", r=RANK),
             )
 
-        def turn_and_group_w_up():
+        def turn_and_group_w_up(banks):
             wu_grouped_rows = wu_grouped[:].rearrange("m (p j) t -> m p j t", j=ROWS_PER_PARTITION)
-            for b in range(ROWS_PER_PARTITION // 2):
+            for b in banks:
                 wu_turned = turned_banks.tile([P, 2, PAIR_TILES, P], BF16, tag="turned")
                 for jj in range(2):
                     for t in range(PAIR_TILES):
@@ -235,44 +235,47 @@ def tile_spokelayer_e_kernel(tc, h, w_down_words, w_down_scales, w_up, gate_bias
                     done = slice((c - 1) * D_CHUNK, (c + 1) * D_CHUNK)
                     nc.sync.dma_start(out=out_rows[i * P:(i + 1) * P, done], in_=result[:, done])
 
-        for i in range(LEAD):
+        for i in range(AHEAD):
             sum_squares(i)
-        for i in range(LEAD):
+        for i in range(2):
             normalise(i)
             turn(i)
             sort_w_up(2 * i)
             sort_w_up(2 * i + 1)
         move_w_down_scales()
-        for i in range(LEAD):
-            collect(i)
-            quantise_h(i)
-        turn_and_group_w_up()
-        project_down(0)
-        silu(0)
-        project_down(1)
-        sum_squares(2)
-        quantise_w_up()
-        silu(1)
-        quantise_view(0)
-        quantise_view(1)
-        project_up(0)
-        sum_squares(3)
+        collect(0)
+        quantise_h(0)
         normalise(2)
+        collect(1)
+        quantise_h(1)
+        turn_and_group_w_up(range(0, 4))
+        project_down(0)
+        sum_squares(3)
+        silu(0)
+        turn_and_group_w_up(range(4, 8))
+        project_down(1)
         turn(2)
-        finish(0)
-        project_up(1)
+        sum_squares(4)
+        quantise_w_up()
+        quantise_view(0)
+        project_up(0)
 
-        for n in range(LEAD, TOKEN_TILES):
-            collect(n)
-            quantise_h(n)
-            project_down(n)
+        for n in range(2, TOKEN_TILES + 2):
             if n + 1 < TOKEN_TILES:
                 normalise(n + 1)
+            if n < TOKEN_TILES:
+                collect(n)
+            if n + 1 < TOKEN_TILES:
                 turn(n + 1)
-            finish(n - 1)
-            if n + 2 < TOKEN_TILES:
-                sum_squares(n + 2)
-            silu(n)
-            quantise_view(n)
-            project_up(n)
-        finish(TOKEN_TILES - 1)
+            if n - 1 < TOKEN_TILES:
+                silu(n - 1)
+            if n < TOKEN_TILES:
+                quantise_h(n)
+                project_down(n)
+            if n - 1 < TOKEN_TILES:
+                quantise_view(n - 1)
+            finish(n - 2)
+            if n - 1 < TOKEN_TILES:
+                project_up(n - 1)
+            if n + AHEAD < TOKEN_TILES:
+                sum_squares(n + AHEAD)

@@ -162,8 +162,9 @@ def tile_spokelayer_e_kernel(tc, h, w_down_words, w_down_scales, w_up, gate_bias
 
         def normalise(i):
             h_norm[i] = work.tile([P, D_MODEL], BF16, tag="h_norm", name="h_norm%d" % i)
-            nc.vector.tensor_scalar(out=h_norm[i][:], in0=h_sb[i][:], scalar1=rstd[i][:, 0:1], scalar2=None,
-                                    op0=ALU.mult)
+            nc.vector.tensor_scalar(out=h_norm[i][:].rearrange("p (u w e) -> p u w e", u=2, e=2),
+                                    in0=h_sb[i][:].rearrange("p (w u e) -> p u w e", u=2, e=2),
+                                    scalar1=rstd[i][:, 0:1], scalar2=None, op0=ALU.mult)
 
         def turn(i):
             h_words = h_norm[i][:].bitcast(F32)
@@ -174,7 +175,7 @@ def tile_spokelayer_e_kernel(tc, h, w_down_words, w_down_scales, w_up, gate_bias
                 for gg in range(2):
                     g = 2 * half + gg
                     for u in range(2):
-                        nc.tensor.transpose(out=bank[:, gg, u, :], in_=h_words[:, 256 * g + u:256 * (g + 1):2],
+                        nc.tensor.transpose(out=bank[:, gg, u, :], in_=h_words[:, 512 * u + P * g:512 * u + P * (g + 1)],
                                             identity=ident_f32[:])
 
         def collect(i):

@@ -27,7 +27,7 @@ D_CHUNK = 512
 D_CHUNKS = D_MODEL // D_CHUNK
 ROWS_PER_PARTITION = D_MODEL // P
 EPS = 2.0 ** -23
-AHEAD = 3
+EARLY = 4
 
 FLOPS = 2 * TOKENS * D_MODEL * PAIRS * 2
 
@@ -39,7 +39,7 @@ def tile_spokelayer_e_kernel(tc, h, w_down_words, w_down_scales, w_up, gate_bias
 
     with ExitStack() as ctx:
         keep = ctx.enter_context(tc.tile_pool(name="keep", bufs=1))
-        work = ctx.enter_context(tc.tile_pool(name="work", bufs=2))
+        work = ctx.enter_context(tc.tile_pool(name="work", bufs=3))
         results = ctx.enter_context(tc.tile_pool(name="results", bufs=3))
         turned_banks = ctx.enter_context(tc.psum_pool(name="turned_banks", bufs=3))
         down_banks = ctx.enter_context(tc.psum_pool(name="down_banks", bufs=1))
@@ -63,13 +63,14 @@ def tile_spokelayer_e_kernel(tc, h, w_down_words, w_down_scales, w_up, gate_bias
 
         gate_raw = keep.tile([P, 1], BF16)
         nc.sync.dma_start(out=gate_raw[:], in_=gate_bias.partition_broadcast(P))
-        for i in range(AHEAD):
+        for i in range(EARLY - 1):
             load_tokens(i)
 
         wu_raw = keep.tile([P, SPOKES, ROWS_PER_PARTITION * RANK], BF16)
         wu_dram = w_up.rearrange("s (p j) r -> p s (j r)", j=ROWS_PER_PARTITION)
         for t in range(PAIR_TILES):
             nc.sync.dma_start(out=wu_raw[:, 2 * t:2 * t + 2, :], in_=wu_dram[:, 2 * t:2 * t + 2, :])
+        load_tokens(EARLY - 1)
 
         wd_scales_raw = keep.tile([P, SPOKES * DOWN_PASSES * RANK], U8, align_bytes=64)
         nc.vector.memset(wd_scales_raw[:].bitcast(I32), 0)
@@ -85,8 +86,11 @@ def tile_spokelayer_e_kernel(tc, h, w_down_words, w_down_scales, w_up, gate_bias
                 out=wd_codes[:, c, :].bitcast(I32).rearrange("p (s n) -> p s n", n=RANK),
                 in_=wd_dram[c],
             )
-        for i in range(AHEAD, TOKEN_TILES):
+        for i in range(EARLY, TOKEN_TILES):
             load_tokens(i)
+
+        silu_warm = keep.tile([P, 1], F32)
+        nc.scalar.activation(out=silu_warm[:], in_=minus_half[:], func=ACT.Silu)
 
         gate_tanh = keep.tile([P, 1], F32)
         nc.scalar.activation(out=gate_tanh[:], in_=gate_raw[:], func=ACT.Tanh, scale=0.5)
@@ -117,12 +121,12 @@ def tile_spokelayer_e_kernel(tc, h, w_down_words, w_down_scales, w_up, gate_bias
         def turn_and_group_w_up(banks):
             wu_grouped_rows = wu_grouped[:].rearrange("m (p j) t -> m p j t", j=ROWS_PER_PARTITION)
             for b in banks:
-                wu_turned = turned_banks.tile([P, 2, PAIR_TILES, P], BF16, tag="turned")
+                wu_turned = up_banks.tile([P, 2, PAIR_TILES, P], BF16, tag="up")
                 for jj in range(2):
                     for t in range(PAIR_TILES):
                         nc.tensor.transpose(out=wu_turned[:, jj, t, :], in_=wu_sorted[:, t, 2 * b + jj, :],
                                             identity=ident_bf16[:])
-                if (b // 2) % 2 == 0:
+                if b % 2 == 0:
                     nc.scalar.copy(out=wu_grouped_rows[:, :, 2 * b:2 * b + 2, :],
                                    in_=wu_turned[:].rearrange("m j t p -> m p j t"))
                 else:
@@ -149,11 +153,17 @@ def tile_spokelayer_e_kernel(tc, h, w_down_words, w_down_scales, w_up, gate_bias
         down = {}
         view = {}
         up = {}
+        result = {}
 
         def sum_squares(i):
-            squares = work.tile([P, D_MODEL], BF16, tag="squares")
             sum_sq = keep.tile([P, 1], F32, name="sum_sq%d" % i)
-            nc.scalar.activation(out=squares[:], in_=h_sb[i][:], func=ACT.Square, accum_out=sum_sq[:])
+            if i == 1:
+                squares = work.tile([P, D_MODEL], BF16, tag="squares_v")
+                nc.vector.scalar_tensor_tensor(out=squares[:], in0=h_sb[i][:], scalar=1.0, in1=h_sb[i][:],
+                                               op0=ALU.mult, op1=ALU.mult, accum_out=sum_sq[:])
+            else:
+                squares = work.tile([P, D_MODEL], BF16, tag="squares_s")
+                nc.scalar.activation(out=squares[:], in_=h_sb[i][:], func=ACT.Square, accum_out=sum_sq[:])
             mean_sq = keep.tile([P, 1], F32, name="mean_sq%d" % i)
             nc.gpsimd.tensor_scalar(out=mean_sq[:], in0=sum_sq[:], scalar1=1.0 / D_MODEL, scalar2=EPS,
                                     op0=ALU.mult, op1=ALU.add)
@@ -226,57 +236,67 @@ def tile_spokelayer_e_kernel(tc, h, w_down_words, w_down_scales, w_up, gate_bias
                     stop=True,
                 )
 
-        def finish(i):
-            result = results.tile([P, D_MODEL], F32, tag="result")
-            for c in range(D_CHUNKS):
+        def finish(i, half):
+            if half == 0:
+                result[i] = results.tile([P, D_MODEL], F32, tag="result", name="result%d" % i)
+            for c in (2 * half, 2 * half + 1):
                 cols = slice(c * D_CHUNK, (c + 1) * D_CHUNK)
-                nc.vector.scalar_tensor_tensor(out=result[:, cols], in0=up[i][c][:], scalar=gate_eighth[:, 0:1],
+                nc.vector.scalar_tensor_tensor(out=result[i][:, cols], in0=up[i][c][:], scalar=gate_eighth[:, 0:1],
                                                in1=h_sb[i][:, cols], op0=ALU.mult, op1=ALU.add)
-                if c % 2 == 1:
-                    done = slice((c - 1) * D_CHUNK, (c + 1) * D_CHUNK)
-                    nc.sync.dma_start(out=out_rows[i * P:(i + 1) * P, done], in_=result[:, done])
+            done = slice(2 * half * D_CHUNK, 2 * (half + 1) * D_CHUNK)
+            nc.sync.dma_start(out=out_rows[i * P:(i + 1) * P, done], in_=result[i][:, done])
 
-        for i in range(AHEAD):
+        for i in range(3):
             sum_squares(i)
-        for i in range(2):
-            normalise(i)
-            turn(i)
-            sort_w_up(2 * i)
-            sort_w_up(2 * i + 1)
-        move_w_down_scales()
+        sort_w_up(0)
+        normalise(0)
+        turn(0)
+        normalise(1)
+        turn(1)
+        for t in range(1, PAIR_TILES):
+            sort_w_up(t)
+        normalise(2)
         collect(0)
         quantise_h(0)
-        normalise(2)
         collect(1)
+        turn_and_group_w_up(range(0, 2))
         quantise_h(1)
-        turn_and_group_w_up(range(0, 4))
-        project_down(0)
+        turn_and_group_w_up(range(2, 4))
         sum_squares(3)
-        silu(0)
         turn_and_group_w_up(range(4, 8))
-        project_down(1)
+        move_w_down_scales()
         turn(2)
+        project_down(0)
+        collect(2)
+        silu(0)
+        normalise(3)
+        turn(3)
         sum_squares(4)
+        project_down(1)
         quantise_w_up()
         quantise_view(0)
+        quantise_h(2)
+        silu(1)
         project_up(0)
 
-        for n in range(2, TOKEN_TILES + 2):
-            if n + 1 < TOKEN_TILES:
-                normalise(n + 1)
-            if n < TOKEN_TILES:
-                collect(n)
-            if n + 1 < TOKEN_TILES:
-                turn(n + 1)
-            if n - 1 < TOKEN_TILES:
-                silu(n - 1)
-            if n < TOKEN_TILES:
-                quantise_h(n)
-                project_down(n)
-            if n - 1 < TOKEN_TILES:
-                quantise_view(n - 1)
-            finish(n - 2)
-            if n - 1 < TOKEN_TILES:
-                project_up(n - 1)
-            if n + AHEAD < TOKEN_TILES:
-                sum_squares(n + AHEAD)
+        for m in range(TOKEN_TILES):
+            if m + 3 < TOKEN_TILES:
+                collect(m + 3)
+            if m + 5 < TOKEN_TILES:
+                sum_squares(m + 5)
+            finish(m, 0)
+            if m + 1 < TOKEN_TILES:
+                quantise_view(m + 1)
+            finish(m, 1)
+            if m + 4 < TOKEN_TILES:
+                normalise(m + 4)
+            if m + 3 < TOKEN_TILES:
+                quantise_h(m + 3)
+            if m + 2 < TOKEN_TILES:
+                project_down(m + 2)
+            if m + 1 < TOKEN_TILES:
+                project_up(m + 1)
+            if m + 4 < TOKEN_TILES:
+                turn(m + 4)
+            if m + 2 < TOKEN_TILES:
+                silu(m + 2)

@@ -48,8 +48,6 @@ def tile_spokelayer_e_kernel(tc, h, w_down_words, w_down_scales, w_up, gate_bias
 
         ident_f32 = keep.tile([P, P], F32)
         make_identity(nc, ident_f32[:])
-        ident_bf16 = keep.tile([P, P], BF16)
-        make_identity(nc, ident_bf16[:])
         minus_half = keep.tile([P, 1], F32)
         nc.gpsimd.memset(minus_half[:], -0.5)
 
@@ -107,31 +105,31 @@ def tile_spokelayer_e_kernel(tc, h, w_down_words, w_down_scales, w_up, gate_bias
                 in_=wd_scales_raw[:].bitcast(I32).rearrange("p (s c w) -> p c s w", c=DOWN_PASSES, s=SPOKES),
             )
 
-        wu_sorted = keep.tile([P, PAIR_TILES, ROWS_PER_PARTITION, P], BF16)
+        wu_sorted = keep.tile([P, 2, ROWS_PER_PARTITION, 2 * P], BF16)
         wu_grouped = keep.tile([P, D_MODEL, PACK], BF16, align_bytes=64)
         wu_codes = keep.tile([P, D_MODEL], U32, align_bytes=64)
         wu_scales = keep.tile([P, D_MODEL], U8, align_bytes=64)
 
-        def sort_w_up(t):
-            nc.vector.tensor_copy(
-                out=wu_sorted[:, t, :, :].rearrange("p j (x r) -> p j x r", x=2),
-                in_=wu_raw[:, 2 * t:2 * t + 2, :].rearrange("p x (j r) -> p j x r", r=RANK),
-            )
+        def sort_w_up(u, x):
+            spokes = wu_raw[:, 4 * u:4 * u + 4, :].rearrange("p (e x) (j r) -> p x j r e", x=2, r=RANK)
+            words = wu_sorted[:, u, :, :].rearrange("p j (x r e) -> p x j r e", x=2, e=2)
+            nc.vector.tensor_copy(out=words[:, x, :, :, :], in_=spokes[:, x, :, :, :])
 
         def turn_and_group_w_up(banks):
-            wu_grouped_rows = wu_grouped[:].rearrange("m (p j) t -> m p j t", j=ROWS_PER_PARTITION)
+            grouped_words = wu_grouped[:].rearrange("m d t -> m (d t)").bitcast(F32).rearrange(
+                "m (p j u) -> m p j u", j=ROWS_PER_PARTITION, u=2)
             for b in banks:
-                wu_turned = up_banks.tile([P, 2, PAIR_TILES, P], BF16, tag="up")
+                wu_turned = up_banks.tile([P, 2, 2, P], F32, tag="up")
                 for jj in range(2):
-                    for t in range(PAIR_TILES):
-                        nc.tensor.transpose(out=wu_turned[:, jj, t, :], in_=wu_sorted[:, t, 2 * b + jj, :],
-                                            identity=ident_bf16[:])
+                    for u in range(2):
+                        words = wu_sorted[:, u, 2 * b + jj, :].bitcast(F32)
+                        nc.tensor.transpose(out=wu_turned[:, jj, u, :], in_=words, identity=ident_f32[:])
                 if b % 2 == 0:
-                    nc.scalar.copy(out=wu_grouped_rows[:, :, 2 * b:2 * b + 2, :],
-                                   in_=wu_turned[:].rearrange("m j t p -> m p j t"))
+                    nc.scalar.copy(out=grouped_words[:, :, 2 * b:2 * b + 2, :],
+                                   in_=wu_turned[:].rearrange("m j u p -> m p j u"))
                 else:
-                    nc.vector.tensor_copy(out=wu_grouped_rows[:, :, 2 * b:2 * b + 2, :],
-                                          in_=wu_turned[:].rearrange("m j t p -> m p j t"))
+                    nc.vector.tensor_copy(out=grouped_words[:, :, 2 * b:2 * b + 2, :],
+                                          in_=wu_turned[:].rearrange("m j u p -> m p j u"))
 
         def quantise_w_up():
             for half in range(2):
@@ -248,13 +246,13 @@ def tile_spokelayer_e_kernel(tc, h, w_down_words, w_down_scales, w_up, gate_bias
 
         for i in range(3):
             sum_squares(i)
-        sort_w_up(0)
         normalise(0)
         turn(0)
         normalise(1)
         turn(1)
-        for t in range(1, PAIR_TILES):
-            sort_w_up(t)
+        for u in range(2):
+            for x in range(2):
+                sort_w_up(u, x)
         normalise(2)
         collect(0)
         quantise_h(0)

@@ -66,8 +66,10 @@ def tile_spokelayer_e_kernel(tc, h, w_down_words, w_down_scales, w_up, gate_bias
 
         wu_raw = keep.tile([P, SPOKES, ROWS_PER_PARTITION * RANK], BF16)
         wu_dram = w_up.rearrange("s (p j) r -> p s (j r)", j=ROWS_PER_PARTITION)
-        for t in range(PAIR_TILES):
-            nc.sync.dma_start(out=wu_raw[:, 2 * t:2 * t + 2, :], in_=wu_dram[:, 2 * t:2 * t + 2, :])
+        for u in range(2):
+            for x in range(2):
+                pair = slice(4 * u + x, 4 * u + x + 3, 2)
+                nc.sync.dma_start(out=wu_raw[:, pair, :], in_=wu_dram[:, pair, :])
         load_tokens(EARLY - 1)
 
         wd_scales_raw = keep.tile([P, SPOKES * DOWN_PASSES * RANK], U8, align_bytes=64)
@@ -244,24 +246,34 @@ def tile_spokelayer_e_kernel(tc, h, w_down_words, w_down_scales, w_up, gate_bias
             done = slice(2 * half * D_CHUNK, 2 * (half + 1) * D_CHUNK)
             nc.sync.dma_start(out=out_rows[i * P:(i + 1) * P, done], in_=result[i][:, done])
 
+        def warm_tensor(count):
+            for k in range(count):
+                nc.tensor.matmul(out=warm[:], lhsT=h_sb[1][:, 0:P], rhs=h_sb[1][:, 0:D_CHUNK], start=True, stop=True)
+
+        warm = down_banks.tile([P, D_CHUNK], F32, tag="down")
         for i in range(3):
             sum_squares(i)
+        warm_tensor(8)
+        sort_w_up(0, 0)
         normalise(0)
         turn(0)
         normalise(1)
         turn(1)
-        for u in range(2):
-            for x in range(2):
-                sort_w_up(u, x)
+        sort_w_up(0, 1)
+        sort_w_up(1, 0)
+        sort_w_up(1, 1)
         normalise(2)
         collect(0)
         quantise_h(0)
         collect(1)
+        sum_squares(3)
+        warm_tensor(5)
         turn_and_group_w_up(range(0, 2))
         quantise_h(1)
-        turn_and_group_w_up(range(2, 4))
-        sum_squares(3)
-        turn_and_group_w_up(range(4, 8))
+        for b in range(2, 8, 2):
+            warm_tensor(1)
+            turn_and_group_w_up(range(b, b + 2))
+        warm_tensor(1)
         move_w_down_scales()
         turn(2)
         project_down(0)

@@ -61,16 +61,21 @@ def tile_spokelayer_e_kernel(tc, h, w_down_words, w_down_scales, w_up, gate_bias
 
         gate_raw = keep.tile([P, 1], BF16)
         nc.sync.dma_start(out=gate_raw[:], in_=gate_bias.partition_broadcast(P))
-        for i in range(EARLY - 1):
-            load_tokens(i)
-
         wu_raw = keep.tile([P, SPOKES, ROWS_PER_PARTITION * RANK], BF16)
         wu_dram = w_up.rearrange("s (p j) r -> p s (j r)", j=ROWS_PER_PARTITION)
-        for u in range(2):
-            for x in range(2):
-                pair = slice(4 * u + x, 4 * u + x + 3, 2)
-                nc.sync.dma_start(out=wu_raw[:, pair, :], in_=wu_dram[:, pair, :])
-        load_tokens(EARLY - 1)
+
+        def load_w_up(u, x):
+            pair = slice(4 * u + x, 4 * u + x + 3, 2)
+            nc.sync.dma_start(out=wu_raw[:, pair, :], in_=wu_dram[:, pair, :])
+
+        load_tokens(0)
+        load_w_up(0, 0)
+        load_tokens(1)
+        load_w_up(0, 1)
+        load_tokens(2)
+        load_w_up(1, 0)
+        load_w_up(1, 1)
+        load_tokens(3)
 
         wd_scales_raw = keep.tile([P, SPOKES * DOWN_PASSES * RANK], U8, align_bytes=64)
         nc.vector.memset(wd_scales_raw[:].bitcast(I32), 0)
@@ -157,13 +162,8 @@ def tile_spokelayer_e_kernel(tc, h, w_down_words, w_down_scales, w_up, gate_bias
 
         def sum_squares(i):
             sum_sq = keep.tile([P, 1], F32, name="sum_sq%d" % i)
-            if i == 1:
-                squares = work.tile([P, D_MODEL], BF16, tag="squares_v")
-                nc.vector.scalar_tensor_tensor(out=squares[:], in0=h_sb[i][:], scalar=1.0, in1=h_sb[i][:],
-                                               op0=ALU.mult, op1=ALU.mult, accum_out=sum_sq[:])
-            else:
-                squares = work.tile([P, D_MODEL], BF16, tag="squares_s")
-                nc.scalar.activation(out=squares[:], in_=h_sb[i][:], func=ACT.Square, accum_out=sum_sq[:])
+            squares = work.tile([P, D_MODEL], BF16, tag="squares")
+            nc.scalar.activation(out=squares[:], in_=h_sb[i][:], func=ACT.Square, accum_out=sum_sq[:])
             mean_sq = keep.tile([P, 1], F32, name="mean_sq%d" % i)
             nc.gpsimd.tensor_scalar(out=mean_sq[:], in0=sum_sq[:], scalar1=1.0 / D_MODEL, scalar2=EPS,
                                     op0=ALU.mult, op1=ALU.add)
@@ -172,9 +172,8 @@ def tile_spokelayer_e_kernel(tc, h, w_down_words, w_down_scales, w_up, gate_bias
 
         def normalise(i):
             h_norm[i] = work.tile([P, D_MODEL], BF16, tag="h_norm", name="h_norm%d" % i)
-            nc.vector.tensor_scalar(out=h_norm[i][:].rearrange("p (u w e) -> p u w e", u=2, e=2),
-                                    in0=h_sb[i][:].rearrange("p (w u e) -> p u w e", u=2, e=2),
-                                    scalar1=rstd[i][:, 0:1], scalar2=None, op0=ALU.mult)
+            nc.vector.tensor_scalar(out=h_norm[i][:], in0=h_sb[i][:], scalar1=rstd[i][:, 0:1], scalar2=None,
+                                    op0=ALU.mult)
 
         def turn(i):
             h_words = h_norm[i][:].bitcast(F32)
@@ -185,7 +184,7 @@ def tile_spokelayer_e_kernel(tc, h, w_down_words, w_down_scales, w_up, gate_bias
                 for gg in range(2):
                     g = 2 * half + gg
                     for u in range(2):
-                        nc.tensor.transpose(out=bank[:, gg, u, :], in_=h_words[:, 512 * u + P * g:512 * u + P * (g + 1)],
+                        nc.tensor.transpose(out=bank[:, gg, u, :], in_=h_words[:, 256 * g + u:256 * (g + 1):2],
                                             identity=ident_f32[:])
 
         def collect(i):
@@ -248,29 +247,32 @@ def tile_spokelayer_e_kernel(tc, h, w_down_words, w_down_scales, w_up, gate_bias
 
         def warm_tensor(count):
             for k in range(count):
-                nc.tensor.matmul(out=warm[:], lhsT=h_sb[1][:, 0:P], rhs=h_sb[1][:, 0:D_CHUNK], start=True, stop=True)
+                nc.tensor.matmul(out=warm[:], lhsT=h_sb[0][:, 0:P], rhs=h_sb[0][:, 0:D_CHUNK], start=True, stop=True)
 
         warm = down_banks.tile([P, D_CHUNK], F32, tag="down")
-        for i in range(3):
+        for i in range(2):
             sum_squares(i)
         warm_tensor(8)
         sort_w_up(0, 0)
         normalise(0)
         turn(0)
-        normalise(1)
-        turn(1)
         sort_w_up(0, 1)
         sort_w_up(1, 0)
+        warm_tensor(5)
+        normalise(1)
+        turn(1)
         sort_w_up(1, 1)
-        normalise(2)
         collect(0)
+        sum_squares(2)
         quantise_h(0)
         collect(1)
-        sum_squares(3)
-        warm_tensor(5)
         turn_and_group_w_up(range(0, 2))
         quantise_h(1)
-        for b in range(2, 8, 2):
+        warm_tensor(1)
+        turn_and_group_w_up(range(2, 4))
+        sum_squares(3)
+        normalise(2)
+        for b in range(4, 8, 2):
             warm_tensor(1)
             turn_and_group_w_up(range(b, b + 2))
         warm_tensor(1)

@@ -53,14 +53,13 @@ def tile_spokelayer_e_kernel(tc, h, w_down_words, w_down_scales, w_up, gate_bias
 
         h_sb = []
         for i in range(TOKEN_TILES):
-            h_tile = keep.tile([P, D_MODEL], BF16, name="h%d" % i)
+            h_tile = keep.tile([P, D_MODEL + 1], BF16, name="h%d" % i)
+            nc.gpsimd.memset(h_tile[:, D_MODEL:D_MODEL + 1], (D_MODEL * EPS) ** 0.5)
             h_sb.append(h_tile)
 
         def load_tokens(i):
-            nc.sync.dma_start(out=h_sb[i][:], in_=h_rows[i * P:(i + 1) * P, :])
+            nc.sync.dma_start(out=h_sb[i][:, 0:D_MODEL], in_=h_rows[i * P:(i + 1) * P, :])
 
-        gate_raw = keep.tile([P, 1], BF16)
-        nc.sync.dma_start(out=gate_raw[:], in_=gate_bias.partition_broadcast(P))
         wu_raw = keep.tile([P, SPOKES, ROWS_PER_PARTITION * RANK], BF16)
         wu_dram = w_up.rearrange("s (p j) r -> p s (j r)", j=ROWS_PER_PARTITION)
 
@@ -69,13 +68,15 @@ def tile_spokelayer_e_kernel(tc, h, w_down_words, w_down_scales, w_up, gate_bias
             nc.sync.dma_start(out=wu_raw[:, pair, :], in_=wu_dram[:, pair, :])
 
         load_tokens(0)
-        load_w_up(0, 0)
         load_tokens(1)
+        load_w_up(0, 0)
         load_w_up(0, 1)
         load_tokens(2)
         load_w_up(1, 0)
         load_w_up(1, 1)
         load_tokens(3)
+        gate_raw = keep.tile([P, 1], BF16)
+        nc.sync.dma_start(out=gate_raw[:], in_=gate_bias.partition_broadcast(P))
 
         wd_scales_raw = keep.tile([P, SPOKES * DOWN_PASSES * RANK], U8, align_bytes=64)
         nc.vector.memset(wd_scales_raw[:].bitcast(I32), 0)
@@ -98,10 +99,14 @@ def tile_spokelayer_e_kernel(tc, h, w_down_words, w_down_scales, w_up, gate_bias
         nc.scalar.activation(out=silu_warm[:], in_=minus_half[:], func=ACT.Silu)
 
         gate_tanh = keep.tile([P, 1], F32)
-        nc.scalar.activation(out=gate_tanh[:], in_=gate_raw[:], func=ACT.Tanh, scale=0.5)
         gate_eighth = keep.tile([P, 1], F32)
-        nc.vector.tensor_scalar(out=gate_eighth[:], in0=gate_tanh[:], scalar1=1.0, scalar2=0.5 / SPOKES,
-                                op0=ALU.add, op1=ALU.mult)
+
+        def make_gate_tanh():
+            nc.scalar.activation(out=gate_tanh[:], in_=gate_raw[:], func=ACT.Tanh, scale=0.5)
+
+        def make_gate():
+            nc.vector.tensor_scalar(out=gate_eighth[:], in0=gate_tanh[:], scalar1=1.0, scalar2=0.5 / SPOKES,
+                                    op0=ALU.add, op1=ALU.mult)
 
         wd_scales = keep.tile([P, DOWN_PASSES, PAIRS], U8, align_bytes=64)
 
@@ -151,7 +156,7 @@ def tile_spokelayer_e_kernel(tc, h, w_down_words, w_down_scales, w_up, gate_bias
         h_scales = keep.tile([P, TOKEN_TILES, DOWN_PASSES * P], U8, align_bytes=64)
         view_codes = keep.tile([P, TOKEN_TILES, P], U32, align_bytes=64)
         view_scales = keep.tile([P, TOKEN_TILES, P], U8, align_bytes=64)
-        rstd = {}
+        rnorm = {}
         h_norm = {}
         h_turned = {}
         h_grouped = {}
@@ -162,18 +167,27 @@ def tile_spokelayer_e_kernel(tc, h, w_down_words, w_down_scales, w_up, gate_bias
 
         def sum_squares(i):
             sum_sq = keep.tile([P, 1], F32, name="sum_sq%d" % i)
-            squares = work.tile([P, D_MODEL], BF16, tag="squares")
-            nc.scalar.activation(out=squares[:], in_=h_sb[i][:], func=ACT.Square, accum_out=sum_sq[:])
-            mean_sq = keep.tile([P, 1], F32, name="mean_sq%d" % i)
-            nc.gpsimd.tensor_scalar(out=mean_sq[:], in0=sum_sq[:], scalar1=1.0 / D_MODEL, scalar2=EPS,
-                                    op0=ALU.mult, op1=ALU.add)
-            rstd[i] = keep.tile([P, 1], F32, name="rstd%d" % i)
-            nc.gpsimd.tensor_tensor(out=rstd[i][:], in0=mean_sq[:], in1=minus_half[:], op=ALU.pow)
+            squares = work.tile([P, D_MODEL + 1], BF16, tag="squares")
+            if i == 0:
+                half = D_MODEL // 2
+                nc.scalar.activation(out=squares[:, 0:half], in_=h_sb[i][:, 0:half], func=ACT.Square,
+                                     accum_out=sum_sq[:])
+                squares_v = work.tile([P, half + 1], BF16, tag="squares_v")
+                sum_sq_v = keep.tile([P, 1], F32)
+                nc.vector.scalar_tensor_tensor(out=squares_v[:], in0=h_sb[i][:, half:], scalar=1.0, in1=h_sb[i][:, half:],
+                                               op0=ALU.mult, op1=ALU.mult, accum_out=sum_sq_v[:])
+                sum_sq_both = keep.tile([P, 1], F32)
+                nc.gpsimd.tensor_tensor(out=sum_sq_both[:], in0=sum_sq[:], in1=sum_sq_v[:], op=ALU.add)
+                sum_sq = sum_sq_both
+            else:
+                nc.scalar.activation(out=squares[:], in_=h_sb[i][:], func=ACT.Square, accum_out=sum_sq[:])
+            rnorm[i] = keep.tile([P, 1], F32, name="rnorm%d" % i)
+            nc.gpsimd.tensor_tensor(out=rnorm[i][:], in0=sum_sq[:], in1=minus_half[:], op=ALU.pow)
 
         def normalise(i):
             h_norm[i] = work.tile([P, D_MODEL], BF16, tag="h_norm", name="h_norm%d" % i)
-            nc.vector.tensor_scalar(out=h_norm[i][:], in0=h_sb[i][:], scalar1=rstd[i][:, 0:1], scalar2=None,
-                                    op0=ALU.mult)
+            nc.vector.tensor_scalar(out=h_norm[i][:], in0=h_sb[i][:, 0:D_MODEL], scalar1=rnorm[i][:, 0:1],
+                                    scalar2=D_MODEL ** 0.5, op0=ALU.mult, op1=ALU.mult)
 
         def turn(i):
             h_words = h_norm[i][:].bitcast(F32)
@@ -242,8 +256,11 @@ def tile_spokelayer_e_kernel(tc, h, w_down_words, w_down_scales, w_up, gate_bias
                 cols = slice(c * D_CHUNK, (c + 1) * D_CHUNK)
                 nc.vector.scalar_tensor_tensor(out=result[i][:, cols], in0=up[i][c][:], scalar=gate_eighth[:, 0:1],
                                                in1=h_sb[i][:, cols], op0=ALU.mult, op1=ALU.add)
-            done = slice(2 * half * D_CHUNK, 2 * (half + 1) * D_CHUNK)
-            nc.sync.dma_start(out=out_rows[i * P:(i + 1) * P, done], in_=result[i][:, done])
+                if i == TOKEN_TILES - 1 and half == 1:
+                    nc.sync.dma_start(out=out_rows[i * P:(i + 1) * P, cols], in_=result[i][:, cols])
+            if i < TOKEN_TILES - 1 or half == 0:
+                done = slice(2 * half * D_CHUNK, 2 * (half + 1) * D_CHUNK)
+                nc.sync.dma_start(out=out_rows[i * P:(i + 1) * P, done], in_=result[i][:, done])
 
         def warm_tensor(count):
             for k in range(count):
@@ -253,9 +270,9 @@ def tile_spokelayer_e_kernel(tc, h, w_down_words, w_down_scales, w_up, gate_bias
         for i in range(2):
             sum_squares(i)
         warm_tensor(8)
-        sort_w_up(0, 0)
         normalise(0)
         turn(0)
+        sort_w_up(0, 0)
         sort_w_up(0, 1)
         sort_w_up(1, 0)
         warm_tensor(5)
@@ -271,6 +288,7 @@ def tile_spokelayer_e_kernel(tc, h, w_down_words, w_down_scales, w_up, gate_bias
         warm_tensor(1)
         turn_and_group_w_up(range(2, 4))
         sum_squares(3)
+        make_gate_tanh()
         normalise(2)
         for b in range(4, 8, 2):
             warm_tensor(1)
@@ -285,6 +303,7 @@ def tile_spokelayer_e_kernel(tc, h, w_down_words, w_down_scales, w_up, gate_bias
         turn(3)
         sum_squares(4)
         project_down(1)
+        make_gate()
         quantise_w_up()
         quantise_view(0)
         quantise_h(2)

@@ -123,9 +123,9 @@ def tile_spokelayer_e_kernel(tc, h, w_down_words, w_down_scales, w_up, gate_bias
         wu_scales = keep.tile([P, D_MODEL], U8, align_bytes=64)
 
         def sort_w_up(u, x):
-            spokes = wu_raw[:, 4 * u:4 * u + 4, :].rearrange("p (e x) (j r) -> p x j r e", x=2, r=RANK)
-            words = wu_sorted[:, u, :, :].rearrange("p j (x r e) -> p x j r e", x=2, e=2)
-            nc.vector.tensor_copy(out=words[:, x, :, :, :], in_=spokes[:, x, :, :, :])
+            spokes = wu_raw[:, 4 * u:4 * u + 4, :].rearrange("p (e x) (j c i) -> p x j c e i", x=2, j=ROWS_PER_PARTITION, i=4)
+            words = wu_sorted[:, u, :, :].rearrange("p j (x c i e) -> p x j c e i", x=2, i=4, e=2)
+            nc.vector.tensor_copy(out=words[:, x, :, :, :, :], in_=spokes[:, x, :, :, :, :])
 
         def turn_and_group_w_up(banks):
             grouped_words = wu_grouped[:].rearrange("m d t -> m (d t)").bitcast(F32).rearrange(

@@ -60,12 +60,12 @@ def tile_spokelayer_e_kernel(tc, h, w_down_words, w_down_scales, w_up, gate_bias
         def load_tokens(i):
             nc.sync.dma_start(out=h_sb[i][:, 0:D_MODEL], in_=h_rows[i * P:(i + 1) * P, :])
 
-        wu_raw = keep.tile([P, SPOKES, ROWS_PER_PARTITION * RANK], BF16)
+        wu_raw = keep.tile([P, 2, 2, 2, ROWS_PER_PARTITION * RANK], BF16)
         wu_dram = w_up.rearrange("s (p j) r -> p s (j r)", j=ROWS_PER_PARTITION)
 
         def load_w_up(u, x):
             pair = slice(4 * u + x, 4 * u + x + 3, 2)
-            nc.sync.dma_start(out=wu_raw[:, pair, :], in_=wu_dram[:, pair, :])
+            nc.sync.dma_start(out=wu_raw[:, u, x, :, :], in_=wu_dram[:, pair, :])
 
         load_tokens(0)
         load_tokens(1)
@@ -123,9 +123,9 @@ def tile_spokelayer_e_kernel(tc, h, w_down_words, w_down_scales, w_up, gate_bias
         wu_scales = keep.tile([P, D_MODEL], U8, align_bytes=64)
 
         def sort_w_up(u, x):
-            spokes = wu_raw[:, 4 * u:4 * u + 4, :].rearrange("p (e x) (j c i) -> p x j c e i", x=2, j=ROWS_PER_PARTITION, i=4)
+            spokes = wu_raw[:, u, x, :, :].rearrange("p e (j c i) -> p j c e i", j=ROWS_PER_PARTITION, i=4)
             words = wu_sorted[:, u, :, :].rearrange("p j (x c i e) -> p x j c e i", x=2, i=4, e=2)
-            nc.vector.tensor_copy(out=words[:, x, :, :, :, :], in_=spokes[:, x, :, :, :, :])
+            nc.vector.tensor_copy(out=words[:, x, :, :, :, :], in_=spokes)
 
         def turn_and_group_w_up(banks):
             grouped_words = wu_grouped[:].rearrange("m d t -> m (d t)").bitcast(F32).rearrange(

from contextlib import ExitStack

import concourse.mybir as mybir
from concourse.masks import make_identity

BF16 = mybir.dt.bfloat16
F32 = mybir.dt.float32
I32 = mybir.dt.int32
U32 = mybir.dt.uint32
U8 = mybir.dt.uint8
FP8X4 = mybir.dt.float8_e4m3fn_x4
ACT = mybir.ActivationFunctionType
ALU = mybir.AluOpType

P = 128
PACK = 4
K_PASS = P * PACK
TOKENS = 1024
D_MODEL = 2048
SPOKES = 8
RANK = 64
PAIRS = SPOKES * RANK
TOKEN_TILES = TOKENS // P
DOWN_PASSES = D_MODEL // K_PASS
PAIR_TILES = PAIRS // P
D_CHUNK = 512
D_CHUNKS = D_MODEL // D_CHUNK
ROWS_PER_PARTITION = D_MODEL // P
EPS = 2.0 ** -23
EARLY = 4

FLOPS = 2 * TOKENS * D_MODEL * PAIRS * 2


def tile_spokelayer_e_kernel(tc, h, w_down_words, w_down_scales, w_up, gate_bias, out):
    nc = tc.nc
    h_rows = h.flatten_outer_dims()
    out_rows = out.flatten_outer_dims()

    with ExitStack() as ctx:
        keep = ctx.enter_context(tc.tile_pool(name="keep", bufs=1))
        work = ctx.enter_context(tc.tile_pool(name="work", bufs=3))
        results = ctx.enter_context(tc.tile_pool(name="results", bufs=3))
        turned_banks = ctx.enter_context(tc.psum_pool(name="turned_banks", bufs=3))
        down_banks = ctx.enter_context(tc.psum_pool(name="down_banks", bufs=1))
        up_banks = ctx.enter_context(tc.psum_pool(name="up_banks", bufs=D_CHUNKS))
        ctx.enter_context(tc.manual_schedule())

        ident_f32 = keep.tile([P, P], F32)
        make_identity(nc, ident_f32[:])
        minus_half = keep.tile([P, 1], F32)
        nc.gpsimd.memset(minus_half[:], -0.5)

        h_sb = []
        for i in range(TOKEN_TILES):
            h_tile = keep.tile([P, D_MODEL + 1], BF16, name="h%d" % i)
            nc.gpsimd.memset(h_tile[:, D_MODEL:D_MODEL + 1], (D_MODEL * EPS) ** 0.5)
            h_sb.append(h_tile)

        def load_tokens(i):
            nc.sync.dma_start(out=h_sb[i][:, 0:D_MODEL], in_=h_rows[i * P:(i + 1) * P, :])

        wu_raw = keep.tile([P, 2, 2, 2, ROWS_PER_PARTITION * RANK], BF16)
        wu_dram = w_up.rearrange("s (p j) r -> p s (j r)", j=ROWS_PER_PARTITION)

        def load_w_up(u, x):
            pair = slice(4 * u + x, 4 * u + x + 3, 2)
            nc.sync.dma_start(out=wu_raw[:, u, x, :, :], in_=wu_dram[:, pair, :])

        load_tokens(0)
        load_tokens(1)
        load_w_up(0, 0)
        load_w_up(0, 1)
        load_tokens(2)
        load_w_up(1, 0)
        load_w_up(1, 1)
        load_tokens(3)
        gate_raw = keep.tile([P, 1], BF16)
        nc.sync.dma_start(out=gate_raw[:], in_=gate_bias.partition_broadcast(P))

        wd_scales_raw = keep.tile([P, SPOKES * DOWN_PASSES * RANK], U8, align_bytes=64)
        nc.vector.memset(wd_scales_raw[:].bitcast(I32), 0)
        for quadrant in range(4):
            nc.sync.dma_start(
                out=wd_scales_raw[32 * quadrant:32 * quadrant + 4, :].bitcast(I32).rearrange("r (g w) -> r g w", w=RANK // 4),
                in_=w_down_scales[:, 4 * quadrant:4 * quadrant + 4, :].bitcast(I32).rearrange("g r w -> r g w"),
            )
        wd_codes = keep.tile([P, DOWN_PASSES, PAIRS], U32, align_bytes=64)
        wd_dram = w_down_words.rearrange("(s c) p n t -> c p s (n t)", c=DOWN_PASSES).bitcast(I32)
        for c in range(DOWN_PASSES):
            nc.sync.dma_start(
                out=wd_codes[:, c, :].bitcast(I32).rearrange("p (s n) -> p s n", n=RANK),
                in_=wd_dram[c],
            )
        for i in range(EARLY, TOKEN_TILES):
            load_tokens(i)

        silu_warm = keep.tile([P, 1], F32)
        nc.scalar.activation(out=silu_warm[:], in_=minus_half[:], func=ACT.Silu)

        gate_tanh = keep.tile([P, 1], F32)
        gate_eighth = keep.tile([P, 1], F32)

        def make_gate_tanh():
            nc.scalar.activation(out=gate_tanh[:], in_=gate_raw[:], func=ACT.Tanh, scale=0.5)

        def make_gate():
            nc.vector.tensor_scalar(out=gate_eighth[:], in0=gate_tanh[:], scalar1=1.0, scalar2=0.5 / SPOKES,
                                    op0=ALU.add, op1=ALU.mult)

        wd_scales = keep.tile([P, DOWN_PASSES, PAIRS], U8, align_bytes=64)

        def move_w_down_scales():
            nc.vector.tensor_copy(
                out=wd_scales[:].rearrange("p c n -> p (c n)").bitcast(I32).rearrange(
                    "p (c s w) -> p c s w", c=DOWN_PASSES, s=SPOKES),
                in_=wd_scales_raw[:].bitcast(I32).rearrange("p (s c w) -> p c s w", c=DOWN_PASSES, s=SPOKES),
            )

        wu_sorted = keep.tile([P, 2, ROWS_PER_PARTITION, 2 * P], BF16)
        wu_grouped = keep.tile([P, D_MODEL, PACK], BF16, align_bytes=64)
        wu_codes = keep.tile([P, D_MODEL], U32, align_bytes=64)
        wu_scales = keep.tile([P, D_MODEL], U8, align_bytes=64)

        def sort_w_up(u, x):
            spokes = wu_raw[:, u, x, :, :].rearrange("p e (j c i) -> p j c e i", j=ROWS_PER_PARTITION, i=4)
            words = wu_sorted[:, u, :, :].rearrange("p j (x c i e) -> p x j c e i", x=2, i=4, e=2)
            nc.vector.tensor_copy(out=words[:, x, :, :, :, :], in_=spokes)

        def turn_and_group_w_up(banks):
            grouped_words = wu_grouped[:].rearrange("m d t -> m (d t)").bitcast(F32).rearrange(
                "m (p j u) -> m p j u", j=ROWS_PER_PARTITION, u=2)
            for b in banks:
                wu_turned = up_banks.tile([P, 2, 2, P], F32, tag="up")
                for jj in range(2):
                    for u in range(2):
                        words = wu_sorted[:, u, 2 * b + jj, :].bitcast(F32)
                        nc.tensor.transpose(out=wu_turned[:, jj, u, :], in_=words, identity=ident_f32[:])
                if b % 2 == 0:
                    nc.scalar.copy(out=grouped_words[:, :, 2 * b:2 * b + 2, :],
                                   in_=wu_turned[:].rearrange("m j u p -> m p j u"))
                else:
                    nc.vector.tensor_copy(out=grouped_words[:, :, 2 * b:2 * b + 2, :],
                                          in_=wu_turned[:].rearrange("m j u p -> m p j u"))

        def quantise_w_up():
            for half in range(2):
                cols = slice(half * D_MODEL // 2, (half + 1) * D_MODEL // 2)
                nc.vector.quantize_mx(
                    out=wu_codes[:, cols].bitcast(FP8X4),
                    scales=wu_scales[:, cols],
                    in_=wu_grouped[:, cols, :].rearrange("m d t -> m (d t)"),
                )

        h_codes = keep.tile([P, TOKEN_TILES, DOWN_PASSES * P], U32, align_bytes=64)
        h_scales = keep.tile([P, TOKEN_TILES, DOWN_PASSES * P], U8, align_bytes=64)
        view_codes = keep.tile([P, TOKEN_TILES, P], U32, align_bytes=64)
        view_scales = keep.tile([P, TOKEN_TILES, P], U8, align_bytes=64)
        rnorm = {}
        h_norm = {}
        h_turned = {}
        h_grouped = {}
        down = {}
        view = {}
        up = {}
        result = {}

        def sum_squares(i):
            sum_sq = keep.tile([P, 1], F32, name="sum_sq%d" % i)
            squares = work.tile([P, D_MODEL + 1], BF16, tag="squares")
            if i == 0:
                half = D_MODEL // 2
                nc.scalar.activation(out=squares[:, 0:half], in_=h_sb[i][:, 0:half], func=ACT.Square,
                                     accum_out=sum_sq[:])
                squares_v = work.tile([P, half + 1], BF16, tag="squares_v")
                sum_sq_v = keep.tile([P, 1], F32)
                nc.vector.scalar_tensor_tensor(out=squares_v[:], in0=h_sb[i][:, half:], scalar=1.0, in1=h_sb[i][:, half:],
                                               op0=ALU.mult, op1=ALU.mult, accum_out=sum_sq_v[:])
                sum_sq_both = keep.tile([P, 1], F32)
                nc.gpsimd.tensor_tensor(out=sum_sq_both[:], in0=sum_sq[:], in1=sum_sq_v[:], op=ALU.add)
                sum_sq = sum_sq_both
            else:
                nc.scalar.activation(out=squares[:], in_=h_sb[i][:], func=ACT.Square, accum_out=sum_sq[:])
            rnorm[i] = keep.tile([P, 1], F32, name="rnorm%d" % i)
            nc.gpsimd.tensor_tensor(out=rnorm[i][:], in0=sum_sq[:], in1=minus_half[:], op=ALU.pow)

        def normalise(i):
            h_norm[i] = work.tile([P, D_MODEL], BF16, tag="h_norm", name="h_norm%d" % i)
            nc.vector.tensor_scalar(out=h_norm[i][:], in0=h_sb[i][:, 0:D_MODEL], scalar1=rnorm[i][:, 0:1],
                                    scalar2=D_MODEL ** 0.5, op0=ALU.mult, op1=ALU.mult)

        def turn(i):
            h_words = h_norm[i][:].bitcast(F32)
            h_turned[i] = []
            for half in range(2):
                bank = turned_banks.tile([P, 2, 2, P], F32, tag="turned", name="h_turned%d_%d" % (i, half))
                h_turned[i].append(bank)
                for gg in range(2):
                    g = 2 * half + gg
                    for u in range(2):
                        nc.tensor.transpose(out=bank[:, gg, u, :], in_=h_words[:, 256 * g + u:256 * (g + 1):2],
                                            identity=ident_f32[:])

        def collect(i):
            h_grouped[i] = work.tile([P, D_MODEL], BF16, tag="h_grouped", name="h_grouped%d" % i, align_bytes=64)
            grouped_words = h_grouped[i][:].bitcast(F32).rearrange("p (g n u) -> p g n u", g=DOWN_PASSES, u=2)
            for half in range(2):
                nc.scalar.copy(out=grouped_words[:, 2 * half:2 * half + 2, :, :],
                               in_=h_turned[i][half][:].rearrange("p g u n -> p g n u"))

        def quantise_h(i):
            nc.vector.quantize_mx(out=h_codes[:, i, :].bitcast(FP8X4), scales=h_scales[:, i, :], in_=h_grouped[i][:])

        def project_down(i):
            down[i] = down_banks.tile([P, PAIR_TILES, P], F32, tag="down", name="down%d" % i)
            for t in range(PAIR_TILES):
                for g in range(DOWN_PASSES):
                    nc.tensor.matmul_mx(
                        out=down[i][:, t, :],
                        lhsT=wd_codes[:, g, t * P:(t + 1) * P].bitcast(FP8X4),
                        lhsT_scale=wd_scales[:, g, t * P:(t + 1) * P],
                        rhs=h_codes[:, i, g * P:(g + 1) * P].bitcast(FP8X4),
                        rhs_scale=h_scales[:, i, g * P:(g + 1) * P],
                        start=(g == 0),
                        stop=(g == DOWN_PASSES - 1),
                    )

        def silu(i):
            view[i] = work.tile([P, P, PACK], BF16, tag="view", name="view%d" % i, align_bytes=64)
            nc.scalar.activation(out=view[i][:], in_=down[i][:].rearrange("m t n -> m n t"), func=ACT.Silu)

        def quantise_view(i):
            nc.vector.quantize_mx(out=view_codes[:, i, :].bitcast(FP8X4), scales=view_scales[:, i, :],
                                  in_=view[i][:].rearrange("m n t -> m (n t)"))

        def project_up(i):
            up[i] = []
            for c in range(D_CHUNKS):
                cols = slice(c * D_CHUNK, (c + 1) * D_CHUNK)
                bank = up_banks.tile([P, D_CHUNK], F32, tag="up", name="up%d_%d" % (i, c))
                up[i].append(bank)
                nc.tensor.matmul_mx(
                    out=bank[:],
                    lhsT=view_codes[:, i, :].bitcast(FP8X4),
                    lhsT_scale=view_scales[:, i, :],
                    rhs=wu_codes[:, cols].bitcast(FP8X4),
                    rhs_scale=wu_scales[:, cols],
                    start=True,
                    stop=True,
                )

        def finish(i, half):
            if half == 0:
                result[i] = results.tile([P, D_MODEL], F32, tag="result", name="result%d" % i)
            for c in (2 * half, 2 * half + 1):
                cols = slice(c * D_CHUNK, (c + 1) * D_CHUNK)
                nc.vector.scalar_tensor_tensor(out=result[i][:, cols], in0=up[i][c][:], scalar=gate_eighth[:, 0:1],
                                               in1=h_sb[i][:, cols], op0=ALU.mult, op1=ALU.add)
                if i == TOKEN_TILES - 1 and half == 1:
                    nc.sync.dma_start(out=out_rows[i * P:(i + 1) * P, cols], in_=result[i][:, cols])
            if i < TOKEN_TILES - 1 or half == 0:
                done = slice(2 * half * D_CHUNK, 2 * (half + 1) * D_CHUNK)
                nc.sync.dma_start(out=out_rows[i * P:(i + 1) * P, done], in_=result[i][:, done])

        def warm_tensor(count):
            for k in range(count):
                nc.tensor.matmul(out=warm[:], lhsT=h_sb[0][:, 0:P], rhs=h_sb[0][:, 0:D_CHUNK], start=True, stop=True)

        warm = down_banks.tile([P, D_CHUNK], F32, tag="down")
        for i in range(2):
            sum_squares(i)
        warm_tensor(8)
        normalise(0)
        turn(0)
        sort_w_up(0, 0)
        sort_w_up(0, 1)
        sort_w_up(1, 0)
        warm_tensor(5)
        normalise(1)
        turn(1)
        sort_w_up(1, 1)
        collect(0)
        sum_squares(2)
        quantise_h(0)
        collect(1)
        turn_and_group_w_up(range(0, 2))
        quantise_h(1)
        warm_tensor(1)
        turn_and_group_w_up(range(2, 4))
        sum_squares(3)
        make_gate_tanh()
        normalise(2)
        for b in range(4, 8, 2):
            warm_tensor(1)
            turn_and_group_w_up(range(b, b + 2))
        warm_tensor(1)
        move_w_down_scales()
        turn(2)
        project_down(0)
        collect(2)
        silu(0)
        normalise(3)
        turn(3)
        sum_squares(4)
        project_down(1)
        make_gate()
        quantise_w_up()
        quantise_view(0)
        quantise_h(2)
        silu(1)
        project_up(0)

        for m in range(TOKEN_TILES):
            if m + 3 < TOKEN_TILES:
                collect(m + 3)
            if m + 5 < TOKEN_TILES:
                sum_squares(m + 5)
            finish(m, 0)
            if m + 1 < TOKEN_TILES:
                quantise_view(m + 1)
            finish(m, 1)
            if m + 4 < TOKEN_TILES:
                normalise(m + 4)
            if m + 3 < TOKEN_TILES:
                quantise_h(m + 3)
            if m + 2 < TOKEN_TILES:
                project_down(m + 2)
            if m + 1 < TOKEN_TILES:
                project_up(m + 1)
            if m + 4 < TOKEN_TILES:
                turn(m + 4)
            if m + 2 < TOKEN_TILES:
                silu(m + 2)
